import numpy as np
import ml_dtypes


def mxq(x, axis, fmt="e4m3"):
    dtype, down = {"e4m3": (ml_dtypes.float8_e4m3fn, 7), "e5m2": (ml_dtypes.float8_e5m2, 14)}[fmt]
    v = np.moveaxis(np.asarray(x, np.float32).astype(ml_dtypes.bfloat16).astype(np.float64), axis, -1)
    blocks = v.reshape(v.shape[:-1] + (-1, 32))
    amax = np.abs(blocks).max(-1, keepdims=True)
    byte = np.maximum(np.where(amax > 0, np.frexp(amax)[1] - 1 + 127, 0) - down, 1)
    scale = np.exp2(byte - 127.0)
    codes = (blocks / scale).astype(np.float32).astype(dtype).astype(np.float64)
    return np.moveaxis((codes * scale).reshape(v.shape), -1, axis)


WIDE = False


def mx_kscale(k):
    if not WIDE:
        return np.ones(k)
    levels = np.array([10, -10, 5, -5, 0])
    if k % 512:
        return np.exp2(np.random.permutation(np.resize(levels, k // 32))).repeat(32)
    a = np.empty((k // 512, 16))
    for p in range(k // 512):
        a[p, :8] = np.random.permutation(np.resize(levels, 8))
        for g in range(8):
            far = levels[np.abs(levels - a[p, g]) >= 10]
            a[p, g + 8] = far[np.random.randint(len(far))]
    return np.exp2(a.ravel()).repeat(32)


BF16 = ml_dtypes.bfloat16


def bf(x):
    return np.asarray(x, np.float32).astype(BF16)


def f64(x):
    return np.asarray(x).astype(np.float64)


B, T, V, C, H, R, G = 4, 1024, 512, 512, 4, 128, 512
EPS = 1e-12


def l2norm(u):
    n = np.sqrt(np.sum(u * u, axis=-1, keepdims=True))
    return u / np.maximum(n, EPS)


def setup_inputs():
    s = mx_kscale(V)
    return {"x": bf(np.random.standard_normal((B, T, V)) * s),
            "basis": bf(np.random.standard_normal((V, R)) / s[:, None]),
            "shared_q_w": bf(np.random.standard_normal((V, C)) / np.sqrt(V) / s[:, None]),
            "shared_k_w": bf(np.random.standard_normal((V, C)) / np.sqrt(V) / s[:, None]),
            "v_coeffs": bf(np.random.standard_normal((C, R)) * 3.0 / np.sqrt(V * R))}


def reference(x, basis, shared_q_w, shared_k_w, v_coeffs):
    v_w = f64(basis) @ f64(v_coeffs).T
    xq = mxq(f64(x), 2, "e4m3")
    q = l2norm(xq @ mxq(f64(shared_q_w), 0, "e4m3"))
    k = l2norm(xq @ mxq(f64(shared_k_w), 0, "e4m3"))
    v = xq @ mxq(v_w, 0, "e4m3")
    return q, k, v

@@ -1,0 +1,232 @@
+from contextlib import ExitStack
+
+import concourse.mybir as mybir
+from concourse.masks import make_identity
+
+F32 = mybir.dt.float32
+BF16 = mybir.dt.bfloat16
+U32 = mybir.dt.uint32
+U8 = mybir.dt.uint8
+FP8X4 = mybir.dt.float8_e4m3fn_x4
+ALU = mybir.AluOpType
+ACT = mybir.ActivationFunctionType
+
+P = 128
+PACK = 4
+K = P * PACK
+C = 512
+R = 128
+TOKENS = 4 * 1024
+N_TILES = TOKENS // P
+PAIR = 2
+N_PAIRS = N_TILES // PAIR
+AHEAD = 2
+X_LOAD_TILES = 4
+V_ON_VECTOR = 8
+EPS = 1e-12
+
+FLOPS = 3 * 2 * TOKENS * K * C + 2 * K * C * R
+
+
+def tile_multiheadassociativememory_pa_kernel(
+    tc, x, basis, shared_q_w, shared_k_w, v_coeffs, out_0, out_1, out_2
+):
+    nc = tc.nc
+
+    x_rows = x.flatten_outer_dims().rearrange("(p n) k -> p n k", n=N_TILES)
+    q_rows = out_0.flatten_outer_dims().rearrange("(p n) c -> p n c", n=N_TILES)
+    k_rows = out_1.flatten_outer_dims().rearrange("(p n) c -> p n c", n=N_TILES)
+    v_rows = out_2.flatten_outer_dims().rearrange("(p n) c -> p n c", n=N_TILES)
+
+    with ExitStack() as ctx:
+        keep = ctx.enter_context(tc.tile_pool(name="keep", bufs=1))
+        xq_pool = ctx.enter_context(tc.tile_pool(name="xq", bufs=AHEAD + 2))
+        out_pool = ctx.enter_context(tc.tile_pool(name="outp", bufs=4))
+        norm_pool = ctx.enter_context(tc.tile_pool(name="norm", bufs=4))
+        qk_psum = ctx.enter_context(tc.psum_pool(name="qk", bufs=6))
+        short_psum = ctx.enter_context(tc.psum_pool(name="short", bufs=2))
+        ctx.enter_context(tc.manual_schedule())
+
+        def load_k_rows(rows, width, name):
+            raw = keep.tile([P, PACK, width], BF16, name=name)
+            nc.sync.dma_start(out=raw[:], in_=rows.rearrange("(p t) w -> p t w", t=PACK))
+            return raw
+
+        basis_sb = load_k_rows(basis, R, "basis_sb")
+        coeff_sb = keep.tile([P, C // P, R], BF16)
+        nc.sync.dma_start(out=coeff_sb[:], in_=v_coeffs.rearrange("(a p) r -> p a r", p=P))
+        q_raw = load_k_rows(shared_q_w, C, "q_raw")
+        k_raw = load_k_rows(shared_k_w, C, "k_raw")
+        x_sb = []
+        for load in range(N_TILES // X_LOAD_TILES):
+            x_part = keep.tile([P, X_LOAD_TILES * K], BF16, name="x_sb%d" % load)
+            nc.sync.dma_start(
+                out=x_part[:].rearrange("p (n k) -> p n k", k=K),
+                in_=x_rows[:, load * X_LOAD_TILES : (load + 1) * X_LOAD_TILES, :],
+            )
+            x_sb.append(x_part)
+
+        ident_bf16 = keep.tile([P, P], BF16)
+        make_identity(nc, ident_bf16[:])
+        ident_f32 = keep.tile([P, P], F32)
+        make_identity(nc, ident_f32[:])
+        minus_half = keep.tile([P, 2], F32)
+        nc.gpsimd.memset(minus_half[:], -0.5)
+
+        def transpose_pair(pair):
+            turned = short_psum.tile([P, PAIR * 2 * P], F32, tag="short")
+            for i in range(PAIR):
+                n = pair * PAIR + i
+                words = x_sb[n // X_LOAD_TILES][:].bitcast(F32)
+                first = (n % X_LOAD_TILES) * (K // 2)
+                for u in range(2):
+                    nc.tensor.transpose(
+                        turned[:, (2 * i + u) * P : (2 * i + u + 1) * P],
+                        words[:, first + u : first + 2 * P : 2],
+                        ident_f32[:],
+                    )
+            return turned
+
+        def regroup_pair(turned, copy):
+            grouped = xq_pool.tile([P, PAIR * P * PACK], BF16, align_bytes=64, name="x_grouped")
+            copy(
+                out=grouped[:].bitcast(F32).rearrange("p (i r u) -> p i r u", i=PAIR, u=2),
+                in_=turned[:].rearrange("p (i u r) -> p i r u", i=PAIR, u=2),
+            )
+            return grouped
+
+        def quantise_pair(grouped):
+            codes = xq_pool.tile([P, PAIR * P], U32, align_bytes=64, name="x_codes")
+            scales = xq_pool.tile([P, PAIR * P], U8, align_bytes=64, name="x_scales")
+            nc.vector.quantize_mx(out=codes[:].bitcast(FP8X4), scales=scales[:], in_=grouped[:])
+            return codes, scales
+
+        def regroup_weight(raw, name):
+            grouped = keep.tile([P, C, PACK], BF16, align_bytes=64, name=name)
+            nc.vector.tensor_copy(
+                out=grouped[:].rearrange("p (c i) t -> p c t i", i=4),
+                in_=raw[:].rearrange("p t (c i) -> p c t i", i=4),
+            )
+            return grouped
+
+        def quantise_weight(grouped, name):
+            codes = keep.tile([P, C], U32, align_bytes=64, name=name + "_codes")
+            scales = keep.tile([P, C], U8, align_bytes=64, name=name + "_scales")
+            nc.vector.quantize_mx(
+                out=codes[:].bitcast(FP8X4),
+                scales=scales[:],
+                in_=grouped[:].rearrange("p c t -> p (c t)"),
+            )
+            return codes, scales
+
+        factors_ps = short_psum.tile([P, 2 * PACK, P], BF16, tag="short")
+        for t in range(PACK):
+            nc.tensor.transpose(factors_ps[:, t, :], basis_sb[:, t, :], ident_bf16[:])
+        for a in range(C // P):
+            nc.tensor.transpose(factors_ps[:, PACK + a, :], coeff_sb[:, a, :], ident_bf16[:])
+        factors = keep.tile([P, 2 * PACK, P], BF16)
+        nc.vector.tensor_copy(out=factors[:], in_=factors_ps[:])
+
+        v_grouped = keep.tile([P, C, PACK], BF16, align_bytes=64)
+        for a in range(C // P):
+            v_w_ps = qk_psum.tile([P, P, PACK], F32, tag="qk")
+            for t in range(PACK):
+                nc.tensor.matmul(
+                    v_w_ps[:, :, t],
+                    lhsT=factors[:, t, :],
+                    rhs=factors[:, PACK + a, :],
+                    start=True,
+                    stop=True,
+                )
+            nc.scalar.copy(out=v_grouped[:, a * P : (a + 1) * P, :], in_=v_w_ps[:])
+
+        q_grouped = regroup_weight(q_raw, "q_grouped")
+        k_grouped = regroup_weight(k_raw, "k_grouped")
+        q_mx = quantise_weight(q_grouped, "q")
+        k_mx = quantise_weight(k_grouped, "k")
+
+        x_mx = {}
+        x_grouped = regroup_pair(transpose_pair(0), nc.scalar.copy)
+        x_mx[0] = quantise_pair(x_grouped)
+        x_grouped = regroup_pair(transpose_pair(1), nc.vector.tensor_copy)
+        v_mx = quantise_weight(v_grouped, "v")
+        x_mx[1] = quantise_pair(x_grouped)
+
+        def product(psum, tag, weight_mx, n):
+            codes, scales = x_mx[n // PAIR]
+            cols = slice((n % PAIR) * P, (n % PAIR + 1) * P)
+            acc = psum.tile([P, C], F32, tag=tag)
+            nc.tensor.matmul_mx(
+                out=acc[:],
+                lhsT=codes[:, cols].bitcast(FP8X4),
+                lhsT_scale=scales[:, cols],
+                rhs=weight_mx[0][:].bitcast(FP8X4),
+                rhs_scale=weight_mx[1][:],
+                start=True,
+                stop=True,
+            )
+            return acc
+
+        out_sb = {}
+        waiting = {}
+        later = {}
+
+        def multiply_and_sum(n):
+            pair, i = divmod(n, PAIR)
+            if i == 0:
+                q_out = out_pool.tile([P, PAIR, C], F32)
+                k_out = out_pool.tile([P, PAIR, C], F32)
+                v_out = out_pool.tile([P, PAIR, C], F32)
+                out_sb[pair] = (q_out, k_out, v_out)
+            q_ps = product(qk_psum, "qk", q_mx, n)
+            k_ps = product(qk_psum, "qk", k_mx, n)
+            v_ps = product(short_psum, "short", v_mx, n)
+            if i == 0 and pair + AHEAD < N_PAIRS:
+                later["turned"] = transpose_pair(pair + AHEAD)
+
+            sumsq = norm_pool.tile([P, 2], F32)
+            q_sq = norm_pool.tile([P, C], BF16)
+            nc.scalar.activation(out=q_sq[:], in_=q_ps[:], func=ACT.Square, accum_out=sumsq[:, 0:1])
+            k_sq = norm_pool.tile([P, C], BF16)
+            nc.scalar.activation(out=k_sq[:], in_=k_ps[:], func=ACT.Square, accum_out=sumsq[:, 1:2])
+            if n % V_ON_VECTOR == V_ON_VECTOR - 1:
+                nc.vector.tensor_copy(out=out_sb[pair][2][:, i, :], in_=v_ps[:])
+            else:
+                nc.scalar.copy(out=out_sb[pair][2][:, i, :], in_=v_ps[:])
+            inv_sqrt = norm_pool.tile([P, 2], F32)
+            nc.gpsimd.tensor_tensor(out=inv_sqrt[:], in0=sumsq[:], in1=minus_half[:], op=ALU.pow)
+            waiting[n] = (q_ps, k_ps, inv_sqrt)
+
+        def prepare_later_pair(n):
+            pair, i = divmod(n, PAIR)
+            if pair + AHEAD < N_PAIRS:
+                if i == 0:
+                    later["grouped"] = regroup_pair(later["turned"], nc.vector.tensor_copy)
+                else:
+                    x_mx[pair + AHEAD] = quantise_pair(later["grouped"])
+
+        def store(n, count):
+            q_out, k_out, v_out = out_sb[n // PAIR]
+            tiles = slice(n + 1 - count, n + 1)
+            part = slice(n % PAIR + 1 - count, n % PAIR + 1)
+            nc.sync.dma_start(out=v_rows[:, tiles, :], in_=v_out[:, part, :])
+            nc.sync.dma_start(out=q_rows[:, tiles, :], in_=q_out[:, part, :])
+            nc.sync.dma_start(out=k_rows[:, tiles, :], in_=k_out[:, part, :])
+
+        for n in range(N_TILES + 1):
+            if n < N_TILES:
+                multiply_and_sum(n)
+            if n > 0:
+                q_ps, k_ps, inv_sqrt = waiting[n - 1]
+                inv_norm = norm_pool.tile([P, 2], F32)
+                nc.vector.tensor_scalar_min(out=inv_norm[:], in0=inv_sqrt[:], scalar1=1.0 / EPS)
+            if n < N_TILES:
+                prepare_later_pair(n)
+            if n > 0:
+                pair, i = divmod(n - 1, PAIR)
+                nc.vector.tensor_scalar_mul(out=out_sb[pair][0][:, i, :], in0=q_ps[:], scalar1=inv_norm[:, 0:1])
+                nc.vector.tensor_scalar_mul(out=out_sb[pair][1][:, i, :], in0=k_ps[:], scalar1=inv_norm[:, 1:2])
+                if pair == 0 or pair == N_PAIRS - 1:
+                    store(n - 1, 1)
+                elif i == PAIR - 1:
+                    store(n - 1, PAIR)

@@ -55,16 +55,23 @@ def tile_multiheadassociativememory_pa_kernel(
         basis_sb = load_k_rows(basis, R, "basis_sb")
         coeff_sb = keep.tile([P, C // P, R], BF16)
         nc.sync.dma_start(out=coeff_sb[:], in_=v_coeffs.rearrange("(a p) r -> p a r", p=P))
-        q_raw = load_k_rows(shared_q_w, C, "q_raw")
-        k_raw = load_k_rows(shared_k_w, C, "k_raw")
-        x_sb = []
-        for load in range(N_TILES // X_LOAD_TILES):
-            x_part = keep.tile([P, X_LOAD_TILES * K], BF16, name="x_sb%d" % load)
+        x_sb = {}
+
+        def load_x(first, count):
+            x_part = keep.tile([P, count * K], BF16, name="x_sb%d" % first)
             nc.sync.dma_start(
                 out=x_part[:].rearrange("p (n k) -> p n k", k=K),
-                in_=x_rows[:, load * X_LOAD_TILES : (load + 1) * X_LOAD_TILES, :],
+                in_=x_rows[:, first : first + count, :],
             )
-            x_sb.append(x_part)
+            for n in range(count):
+                x_sb[first + n] = (x_part, n)
+
+        load_x(0, PAIR)
+        q_raw = load_k_rows(shared_q_w, C, "q_raw")
+        k_raw = load_k_rows(shared_k_w, C, "k_raw")
+        load_x(PAIR, X_LOAD_TILES - PAIR)
+        for first in range(X_LOAD_TILES, N_TILES, X_LOAD_TILES):
+            load_x(first, X_LOAD_TILES)
 
         ident_bf16 = keep.tile([P, P], BF16)
         make_identity(nc, ident_bf16[:])
@@ -77,8 +84,9 @@ def tile_multiheadassociativememory_pa_kernel(
             turned = short_psum.tile([P, PAIR * 2 * P], F32, tag="short")
             for i in range(PAIR):
                 n = pair * PAIR + i
-                words = x_sb[n // X_LOAD_TILES][:].bitcast(F32)
-                first = (n % X_LOAD_TILES) * (K // 2)
+                x_part, place = x_sb[n]
+                words = x_part[:].bitcast(F32)
+                first = place * (K // 2)
                 for u in range(2):
                     nc.tensor.transpose(
                         turned[:, (2 * i + u) * P : (2 * i + u + 1) * P],
@@ -127,6 +135,8 @@ def tile_multiheadassociativememory_pa_kernel(
         factors = keep.tile([P, 2 * PACK, P], BF16)
         nc.vector.tensor_copy(out=factors[:], in_=factors_ps[:])
 
+        x_grouped = regroup_pair(transpose_pair(0), nc.scalar.copy)
+
         v_grouped = keep.tile([P, C, PACK], BF16, align_bytes=64)
         for a in range(C // P):
             v_w_ps = qk_psum.tile([P, P, PACK], F32, tag="qk")
@@ -140,17 +150,13 @@ def tile_multiheadassociativememory_pa_kernel(
                 )
             nc.scalar.copy(out=v_grouped[:, a * P : (a + 1) * P, :], in_=v_w_ps[:])
 
-        q_grouped = regroup_weight(q_raw, "q_grouped")
-        k_grouped = regroup_weight(k_raw, "k_grouped")
-        q_mx = quantise_weight(q_grouped, "q")
-        k_mx = quantise_weight(k_grouped, "k")
-
         x_mx = {}
-        x_grouped = regroup_pair(transpose_pair(0), nc.scalar.copy)
+        q_grouped = regroup_weight(q_raw, "q_grouped")
         x_mx[0] = quantise_pair(x_grouped)
-        x_grouped = regroup_pair(transpose_pair(1), nc.vector.tensor_copy)
+        q_mx = quantise_weight(q_grouped, "q")
+        k_grouped = regroup_weight(k_raw, "k_grouped")
         v_mx = quantise_weight(v_grouped, "v")
-        x_mx[1] = quantise_pair(x_grouped)
+        k_mx = quantise_weight(k_grouped, "k")
 
         def product(psum, tag, weight_mx, n):
             codes, scales = x_mx[n // PAIR]
@@ -168,42 +174,45 @@ def tile_multiheadassociativememory_pa_kernel(
             return acc
 
         out_sb = {}
-        waiting = {}
-        later = {}
+        qk_ps = {}
+        sums = {}
+        inv_norms = {}
 
-        def multiply_and_sum(n):
+        def open_pair(pair):
+            q_out = out_pool.tile([P, PAIR, C], F32)
+            k_out = out_pool.tile([P, PAIR, C], F32)
+            v_out = out_pool.tile([P, PAIR, C], F32)
+            out_sb[pair] = (q_out, k_out, v_out)
+
+        def sum_of_squares(n, which):
+            if n not in sums:
+                sumsq = norm_pool.tile([P, 2], F32)
+                sums[n] = sumsq
+            squares = norm_pool.tile([P, C], BF16)
+            nc.scalar.activation(
+                out=squares[:], in_=qk_ps[n][which][:], func=ACT.Square, accum_out=sums[n][:, which : which + 1]
+            )
+
+        def invert_norms(n):
+            bounded = norm_pool.tile([P, 2], F32)
+            nc.gpsimd.tensor_scalar_max(out=bounded[:], in0=sums[n][:], scalar1=EPS * EPS)
+            inv_norm = norm_pool.tile([P, 2], F32)
+            nc.gpsimd.tensor_tensor(out=inv_norm[:], in0=bounded[:], in1=minus_half[:], op=ALU.pow)
+            inv_norms[n] = inv_norm
+
+        def scale(n):
             pair, i = divmod(n, PAIR)
-            if i == 0:
-                q_out = out_pool.tile([P, PAIR, C], F32)
-                k_out = out_pool.tile([P, PAIR, C], F32)
-                v_out = out_pool.tile([P, PAIR, C], F32)
-                out_sb[pair] = (q_out, k_out, v_out)
-            q_ps = product(qk_psum, "qk", q_mx, n)
-            k_ps = product(qk_psum, "qk", k_mx, n)
-            v_ps = product(short_psum, "short", v_mx, n)
-            if i == 0 and pair + AHEAD < N_PAIRS:
-                later["turned"] = transpose_pair(pair + AHEAD)
-
-            sumsq = norm_pool.tile([P, 2], F32)
-            q_sq = norm_pool.tile([P, C], BF16)
-            nc.scalar.activation(out=q_sq[:], in_=q_ps[:], func=ACT.Square, accum_out=sumsq[:, 0:1])
-            k_sq = norm_pool.tile([P, C], BF16)
-            nc.scalar.activation(out=k_sq[:], in_=k_ps[:], func=ACT.Square, accum_out=sumsq[:, 1:2])
-            if n % V_ON_VECTOR == V_ON_VECTOR - 1:
-                nc.vector.tensor_copy(out=out_sb[pair][2][:, i, :], in_=v_ps[:])
-            else:
-                nc.scalar.copy(out=out_sb[pair][2][:, i, :], in_=v_ps[:])
-            inv_sqrt = norm_pool.tile([P, 2], F32)
-            nc.gpsimd.tensor_tensor(out=inv_sqrt[:], in0=sumsq[:], in1=minus_half[:], op=ALU.pow)
-            waiting[n] = (q_ps, k_ps, inv_sqrt)
-
-        def prepare_later_pair(n):
-            pair, i = divmod(n, PAIR)
-            if pair + AHEAD < N_PAIRS:
-                if i == 0:
-                    later["grouped"] = regroup_pair(later["turned"], nc.vector.tensor_copy)
+            for which in range(2):
+                out = out_sb[pair][which][:, i, :]
+                inv_norm = inv_norms[n][:, which : which + 1]
+                if n == N_TILES - 1 and which == 1:
+                    nc.scalar.activation(out=out, in_=qk_ps[n][which][:], func=ACT.Copy, scale=inv_norm)
                 else:
-                    x_mx[pair + AHEAD] = quantise_pair(later["grouped"])
+                    nc.vector.tensor_scalar_mul(out=out, in0=qk_ps[n][which][:], scalar1=inv_norm)
+
+        def copy_v(copy, n, v_ps):
+            pair, i = divmod(n, PAIR)
+            copy(out=out_sb[pair][2][:, i, :], in_=v_ps[:])
 
         def store(n, count):
             q_out, k_out, v_out = out_sb[n // PAIR]
@@ -213,20 +222,49 @@ def tile_multiheadassociativememory_pa_kernel(
             nc.sync.dma_start(out=q_rows[:, tiles, :], in_=q_out[:, part, :])
             nc.sync.dma_start(out=k_rows[:, tiles, :], in_=k_out[:, part, :])
 
-        for n in range(N_TILES + 1):
-            if n < N_TILES:
-                multiply_and_sum(n)
-            if n > 0:
-                q_ps, k_ps, inv_sqrt = waiting[n - 1]
-                inv_norm = norm_pool.tile([P, 2], F32)
-                nc.vector.tensor_scalar_min(out=inv_norm[:], in0=inv_sqrt[:], scalar1=1.0 / EPS)
-            if n < N_TILES:
-                prepare_later_pair(n)
-            if n > 0:
-                pair, i = divmod(n - 1, PAIR)
-                nc.vector.tensor_scalar_mul(out=out_sb[pair][0][:, i, :], in0=q_ps[:], scalar1=inv_norm[:, 0:1])
-                nc.vector.tensor_scalar_mul(out=out_sb[pair][1][:, i, :], in0=k_ps[:], scalar1=inv_norm[:, 1:2])
-                if pair == 0 or pair == N_PAIRS - 1:
-                    store(n - 1, 1)
-                elif i == PAIR - 1:
-                    store(n - 1, PAIR)
+        open_pair(0)
+        first_q = [product(qk_psum, "qk", q_mx, n) for n in range(PAIR)]
+        turned = transpose_pair(1)
+        v_ps = product(short_psum, "short", v_mx, 0)
+        first_k = [product(qk_psum, "qk", k_mx, n) for n in range(PAIR)]
+        for n in range(PAIR):
+            qk_ps[n] = (first_q[n], first_k[n])
+        for n in range(PAIR):
+            sum_of_squares(n, 0)
+        x_grouped = regroup_pair(turned, nc.scalar.copy)
+        x_mx[1] = quantise_pair(x_grouped)
+        copy_v(nc.scalar.copy, 0, v_ps)
+        v_ps = product(short_psum, "short", v_mx, 1)
+        copy_v(nc.vector.tensor_copy, 1, v_ps)
+        for n in range(PAIR):
+            sum_of_squares(n, 1)
+            invert_norms(n)
+        x_grouped = regroup_pair(transpose_pair(AHEAD), nc.vector.tensor_copy)
+        x_mx[AHEAD] = quantise_pair(x_grouped)
+
+        for n in range(1, N_TILES + 1):
+            pair, i = divmod(n, PAIR)
+            if PAIR <= n < N_TILES:
+                if i == 0:
+                    open_pair(pair)
+                q_ps = product(qk_psum, "qk", q_mx, n)
+                k_ps = product(qk_psum, "qk", k_mx, n)
+                v_ps = product(short_psum, "short", v_mx, n)
+                qk_ps[n] = (q_ps, k_ps)
+                if i == 0 and pair + AHEAD < N_PAIRS:
+                    turned = transpose_pair(pair + AHEAD)
+                sum_of_squares(n, 0)
+                sum_of_squares(n, 1)
+                invert_norms(n)
+                copy_v(nc.vector.tensor_copy if n % V_ON_VECTOR == V_ON_VECTOR - 1 else nc.scalar.copy, n, v_ps)
+                if pair + AHEAD < N_PAIRS:
+                    if i == 0:
+                        x_grouped = regroup_pair(turned, nc.vector.tensor_copy)
+                    else:
+                        x_mx[pair + AHEAD] = quantise_pair(x_grouped)
+            scale(n - 1)
+            pair, i = divmod(n - 1, PAIR)
+            if pair == 0 or pair == N_PAIRS - 1:
+                store(n - 1, 1)
+            elif i == PAIR - 1:
+                store(n - 1, PAIR)

@@ -22,6 +22,7 @@ PAIR = 2
 N_PAIRS = N_TILES // PAIR
 AHEAD = 2
 X_LOAD_TILES = 4
+X_EARLY_TILES = 20
 V_ON_VECTOR = 8
 EPS = 1e-12
 
@@ -70,8 +71,9 @@ def tile_multiheadassociativememory_pa_kernel(
         q_raw = load_k_rows(shared_q_w, C, "q_raw")
         k_raw = load_k_rows(shared_k_w, C, "k_raw")
         load_x(PAIR, X_LOAD_TILES - PAIR)
-        for first in range(X_LOAD_TILES, N_TILES, X_LOAD_TILES):
+        for first in range(X_LOAD_TILES, X_EARLY_TILES, X_LOAD_TILES):
             load_x(first, X_LOAD_TILES)
+        late_loads = list(range(X_EARLY_TILES, N_TILES, X_LOAD_TILES))
 
         ident_bf16 = keep.tile([P, P], BF16)
         make_identity(nc, ident_bf16[:])
@@ -214,13 +216,17 @@ def tile_multiheadassociativememory_pa_kernel(
             pair, i = divmod(n, PAIR)
             copy(out=out_sb[pair][2][:, i, :], in_=v_ps[:])
 
-        def store(n, count):
-            q_out, k_out, v_out = out_sb[n // PAIR]
+        def store(n, count, names="vqk"):
             tiles = slice(n + 1 - count, n + 1)
             part = slice(n % PAIR + 1 - count, n % PAIR + 1)
-            nc.sync.dma_start(out=v_rows[:, tiles, :], in_=v_out[:, part, :])
-            nc.sync.dma_start(out=q_rows[:, tiles, :], in_=q_out[:, part, :])
-            nc.sync.dma_start(out=k_rows[:, tiles, :], in_=k_out[:, part, :])
+            for name in names:
+                rows, which = {"q": (q_rows, 0), "k": (k_rows, 1), "v": (v_rows, 2)}[name]
+                nc.sync.dma_start(out=rows[:, tiles, :], in_=out_sb[n // PAIR][which][:, part, :])
+
+        def load_late_x():
+            if late_loads:
+                load_x(late_loads[0], X_LOAD_TILES)
+                late_loads.remove(late_loads[0])
 
         open_pair(0)
         first_q = [product(qk_psum, "qk", q_mx, n) for n in range(PAIR)]
@@ -234,14 +240,19 @@ def tile_multiheadassociativememory_pa_kernel(
         x_grouped = regroup_pair(turned, nc.scalar.copy)
         x_mx[1] = quantise_pair(x_grouped)
         copy_v(nc.scalar.copy, 0, v_ps)
+        store(0, 1, "v")
+        load_late_x()
         v_ps = product(short_psum, "short", v_mx, 1)
         copy_v(nc.vector.tensor_copy, 1, v_ps)
+        store(1, 1, "v")
+        load_late_x()
         for n in range(PAIR):
             sum_of_squares(n, 1)
             invert_norms(n)
         x_grouped = regroup_pair(transpose_pair(AHEAD), nc.vector.tensor_copy)
         x_mx[AHEAD] = quantise_pair(x_grouped)
 
+        last_v = []
         for n in range(1, N_TILES + 1):
             pair, i = divmod(n, PAIR)
             if PAIR <= n < N_TILES:
@@ -256,15 +267,26 @@ def tile_multiheadassociativememory_pa_kernel(
                 sum_of_squares(n, 0)
                 sum_of_squares(n, 1)
                 invert_norms(n)
-                copy_v(nc.vector.tensor_copy if n % V_ON_VECTOR == V_ON_VECTOR - 1 else nc.scalar.copy, n, v_ps)
+                if pair == N_PAIRS - 1:
+                    last_v.append(v_ps)
+                elif n % V_ON_VECTOR == V_ON_VECTOR - 1:
+                    copy_v(nc.vector.tensor_copy, n, v_ps)
+                else:
+                    copy_v(nc.scalar.copy, n, v_ps)
                 if pair + AHEAD < N_PAIRS:
                     if i == 0:
                         x_grouped = regroup_pair(turned, nc.vector.tensor_copy)
                     else:
                         x_mx[pair + AHEAD] = quantise_pair(x_grouped)
+            if n == N_TILES - 1:
+                for i in range(PAIR):
+                    copy_v(nc.scalar.copy, n - 1 + i, last_v[i])
             scale(n - 1)
             pair, i = divmod(n - 1, PAIR)
-            if pair == 0 or pair == N_PAIRS - 1:
+            if pair == 0:
+                store(n - 1, 1, "qk")
+                load_late_x()
+            elif pair == N_PAIRS - 1:
                 store(n - 1, 1)
             elif i == PAIR - 1:
                 store(n - 1, PAIR)

@@ -22,7 +22,7 @@ PAIR = 2
 N_PAIRS = N_TILES // PAIR
 AHEAD = 2
 X_LOAD_TILES = 4
-X_EARLY_TILES = 20
+X_EARLY_TILES = 24
 V_ON_VECTOR = 8
 EPS = 1e-12
 
@@ -44,7 +44,7 @@ def tile_multiheadassociativememory_pa_kernel(
         xq_pool = ctx.enter_context(tc.tile_pool(name="xq", bufs=AHEAD + 2))
         out_pool = ctx.enter_context(tc.tile_pool(name="outp", bufs=4))
         norm_pool = ctx.enter_context(tc.tile_pool(name="norm", bufs=4))
-        qk_psum = ctx.enter_context(tc.psum_pool(name="qk", bufs=6))
+        qk_psum = ctx.enter_context(tc.psum_pool(name="qk", bufs=3))
         short_psum = ctx.enter_context(tc.psum_pool(name="short", bufs=2))
         ctx.enter_context(tc.manual_schedule())
 
@@ -141,7 +141,7 @@ def tile_multiheadassociativememory_pa_kernel(
 
         v_grouped = keep.tile([P, C, PACK], BF16, align_bytes=64)
         for a in range(C // P):
-            v_w_ps = qk_psum.tile([P, P, PACK], F32, tag="qk")
+            v_w_ps = qk_psum.tile([P, P, PACK], F32, tag="qk"[a % 2])
             for t in range(PACK):
                 nc.tensor.matmul(
                     v_w_ps[:, :, t],
@@ -229,10 +229,10 @@ def tile_multiheadassociativememory_pa_kernel(
                 late_loads.remove(late_loads[0])
 
         open_pair(0)
-        first_q = [product(qk_psum, "qk", q_mx, n) for n in range(PAIR)]
+        first_q = [product(qk_psum, "q", q_mx, n) for n in range(PAIR)]
         turned = transpose_pair(1)
         v_ps = product(short_psum, "short", v_mx, 0)
-        first_k = [product(qk_psum, "qk", k_mx, n) for n in range(PAIR)]
+        first_k = [product(qk_psum, "k", k_mx, n) for n in range(PAIR)]
         for n in range(PAIR):
             qk_ps[n] = (first_q[n], first_k[n])
         for n in range(PAIR):
@@ -258,8 +258,8 @@ def tile_multiheadassociativememory_pa_kernel(
             if PAIR <= n < N_TILES:
                 if i == 0:
                     open_pair(pair)
-                q_ps = product(qk_psum, "qk", q_mx, n)
-                k_ps = product(qk_psum, "qk", k_mx, n)
+                q_ps = product(qk_psum, "q", q_mx, n)
+                k_ps = product(qk_psum, "k", k_mx, n)
                 v_ps = product(short_psum, "short", v_mx, n)
                 qk_ps[n] = (q_ps, k_ps)
                 if i == 0 and pair + AHEAD < N_PAIRS:

@@ -20,6 +20,7 @@ TOKENS = 4 * 1024
 N_TILES = TOKENS // P
 PAIR = 2
 N_PAIRS = N_TILES // PAIR
+OUT_PAIRS = 10
 AHEAD = 2
 X_LOAD_TILES = 4
 X_EARLY_TILES = 24
@@ -42,8 +43,9 @@ def tile_multiheadassociativememory_pa_kernel(
     with ExitStack() as ctx:
         keep = ctx.enter_context(tc.tile_pool(name="keep", bufs=1))
         xq_pool = ctx.enter_context(tc.tile_pool(name="xq", bufs=AHEAD + 2))
-        out_pool = ctx.enter_context(tc.tile_pool(name="outp", bufs=4))
-        norm_pool = ctx.enter_context(tc.tile_pool(name="norm", bufs=4))
+        out_pool = ctx.enter_context(tc.tile_pool(name="outp", bufs=OUT_PAIRS))
+        square_pool = ctx.enter_context(tc.tile_pool(name="square", bufs=16))
+        norm_pool = ctx.enter_context(tc.tile_pool(name="norm", bufs=N_TILES))
         qk_psum = ctx.enter_context(tc.psum_pool(name="qk", bufs=3))
         short_psum = ctx.enter_context(tc.psum_pool(name="short", bufs=2))
         ctx.enter_context(tc.manual_schedule())
@@ -67,8 +69,8 @@ def tile_multiheadassociativememory_pa_kernel(
             for n in range(count):
                 x_sb[first + n] = (x_part, n)
 
-        load_x(0, PAIR)
         q_raw = load_k_rows(shared_q_w, C, "q_raw")
+        load_x(0, PAIR)
         k_raw = load_k_rows(shared_k_w, C, "k_raw")
         load_x(PAIR, X_LOAD_TILES - PAIR)
         for first in range(X_LOAD_TILES, X_EARLY_TILES, X_LOAD_TILES):
@@ -129,15 +131,16 @@ def tile_multiheadassociativememory_pa_kernel(
             )
             return codes, scales
 
-        factors_ps = short_psum.tile([P, 2 * PACK, P], BF16, tag="short")
+        basis_ps = qk_psum.tile([P, PACK, P], BF16, tag="q")
         for t in range(PACK):
-            nc.tensor.transpose(factors_ps[:, t, :], basis_sb[:, t, :], ident_bf16[:])
+            nc.tensor.transpose(basis_ps[:, t, :], basis_sb[:, t, :], ident_bf16[:])
+        basis_turned = keep.tile([P, PACK, P], BF16)
+        nc.vector.tensor_copy(out=basis_turned[:], in_=basis_ps[:])
+        coeff_ps = short_psum.tile([P, C // P, P], BF16, tag="short")
         for a in range(C // P):
-            nc.tensor.transpose(factors_ps[:, PACK + a, :], coeff_sb[:, a, :], ident_bf16[:])
-        factors = keep.tile([P, 2 * PACK, P], BF16)
-        nc.vector.tensor_copy(out=factors[:], in_=factors_ps[:])
-
-        x_grouped = regroup_pair(transpose_pair(0), nc.scalar.copy)
+            nc.tensor.transpose(coeff_ps[:, a, :], coeff_sb[:, a, :], ident_bf16[:])
+        coeff_turned = keep.tile([P, C // P, P], BF16)
+        nc.vector.tensor_copy(out=coeff_turned[:], in_=coeff_ps[:])
 
         v_grouped = keep.tile([P, C, PACK], BF16, align_bytes=64)
         for a in range(C // P):
@@ -145,17 +148,19 @@ def tile_multiheadassociativememory_pa_kernel(
             for t in range(PACK):
                 nc.tensor.matmul(
                     v_w_ps[:, :, t],
-                    lhsT=factors[:, t, :],
-                    rhs=factors[:, PACK + a, :],
+                    lhsT=basis_turned[:, t, :],
+                    rhs=coeff_turned[:, a, :],
                     start=True,
                     stop=True,
                 )
             nc.scalar.copy(out=v_grouped[:, a * P : (a + 1) * P, :], in_=v_w_ps[:])
+            if a == 0:
+                x_grouped = regroup_pair(transpose_pair(0), nc.scalar.copy)
 
         x_mx = {}
         q_grouped = regroup_weight(q_raw, "q_grouped")
-        x_mx[0] = quantise_pair(x_grouped)
         q_mx = quantise_weight(q_grouped, "q")
+        x_mx[0] = quantise_pair(x_grouped)
         k_grouped = regroup_weight(k_raw, "k_grouped")
         v_mx = quantise_weight(v_grouped, "v")
         k_mx = quantise_weight(k_grouped, "k")
@@ -190,7 +195,7 @@ def tile_multiheadassociativememory_pa_kernel(
             if n not in sums:
                 sumsq = norm_pool.tile([P, 2], F32)
                 sums[n] = sumsq
-            squares = norm_pool.tile([P, C], BF16)
+            squares = square_pool.tile([P, C], BF16)
             nc.scalar.activation(
                 out=squares[:], in_=qk_ps[n][which][:], func=ACT.Square, accum_out=sums[n][:, which : which + 1]
             )

@@ -20,9 +20,10 @@ TOKENS = 4 * 1024
 N_TILES = TOKENS // P
 PAIR = 2
 N_PAIRS = N_TILES // PAIR
-OUT_PAIRS = 10
+OUT_TILES = 2
+STORES = [1, 1] + 15 * [OUT_TILES]
 AHEAD = 2
-X_LOAD_TILES = 4
+X_LOAD_TILES = 8
 X_EARLY_TILES = 24
 V_ON_VECTOR = 8
 EPS = 1e-12
@@ -43,7 +44,7 @@ def tile_multiheadassociativememory_pa_kernel(
     with ExitStack() as ctx:
         keep = ctx.enter_context(tc.tile_pool(name="keep", bufs=1))
         xq_pool = ctx.enter_context(tc.tile_pool(name="xq", bufs=AHEAD + 2))
-        out_pool = ctx.enter_context(tc.tile_pool(name="outp", bufs=OUT_PAIRS))
+        out_pool = ctx.enter_context(tc.tile_pool(name="outp", bufs=10))
         square_pool = ctx.enter_context(tc.tile_pool(name="square", bufs=16))
         norm_pool = ctx.enter_context(tc.tile_pool(name="norm", bufs=N_TILES))
         qk_psum = ctx.enter_context(tc.psum_pool(name="qk", bufs=3))
@@ -56,8 +57,8 @@ def tile_multiheadassociativememory_pa_kernel(
             return raw
 
         basis_sb = load_k_rows(basis, R, "basis_sb")
-        coeff_sb = keep.tile([P, C // P, R], BF16)
-        nc.sync.dma_start(out=coeff_sb[:], in_=v_coeffs.rearrange("(a p) r -> p a r", p=P))
+        coeff_sb = keep.tile([P, PACK, R], BF16)
+        nc.sync.dma_start(out=coeff_sb[:], in_=v_coeffs.rearrange("(p a) r -> p a r", a=PACK))
         x_sb = {}
 
         def load_x(first, count):
@@ -72,7 +73,8 @@ def tile_multiheadassociativememory_pa_kernel(
         q_raw = load_k_rows(shared_q_w, C, "q_raw")
         load_x(0, PAIR)
         k_raw = load_k_rows(shared_k_w, C, "k_raw")
-        load_x(PAIR, X_LOAD_TILES - PAIR)
+        load_x(PAIR, PAIR)
+        load_x(2 * PAIR, X_LOAD_TILES - 2 * PAIR)
         for first in range(X_LOAD_TILES, X_EARLY_TILES, X_LOAD_TILES):
             load_x(first, X_LOAD_TILES)
         late_loads = list(range(X_EARLY_TILES, N_TILES, X_LOAD_TILES))
@@ -136,11 +138,13 @@ def tile_multiheadassociativememory_pa_kernel(
             nc.tensor.transpose(basis_ps[:, t, :], basis_sb[:, t, :], ident_bf16[:])
         basis_turned = keep.tile([P, PACK, P], BF16)
         nc.vector.tensor_copy(out=basis_turned[:], in_=basis_ps[:])
-        coeff_ps = short_psum.tile([P, C // P, P], BF16, tag="short")
-        for a in range(C // P):
+        coeff_ps = short_psum.tile([P, PACK, P], BF16, tag="short")
+        for a in range(PACK):
             nc.tensor.transpose(coeff_ps[:, a, :], coeff_sb[:, a, :], ident_bf16[:])
-        coeff_turned = keep.tile([P, C // P, P], BF16)
-        nc.vector.tensor_copy(out=coeff_turned[:], in_=coeff_ps[:])
+        coeff_turned = keep.tile([P, C], BF16)
+        nc.vector.tensor_copy(
+            out=coeff_turned[:].rearrange("p (c a) -> p c a", a=PACK), in_=coeff_ps[:].rearrange("p a c -> p c a")
+        )
 
         v_grouped = keep.tile([P, C, PACK], BF16, align_bytes=64)
         for a in range(C // P):
@@ -149,7 +153,7 @@ def tile_multiheadassociativememory_pa_kernel(
                 nc.tensor.matmul(
                     v_w_ps[:, :, t],
                     lhsT=basis_turned[:, t, :],
-                    rhs=coeff_turned[:, a, :],
+                    rhs=coeff_turned[:, a * P : (a + 1) * P],
                     start=True,
                     stop=True,
                 )
@@ -185,11 +189,20 @@ def tile_multiheadassociativememory_pa_kernel(
         sums = {}
         inv_norms = {}
 
-        def open_pair(pair):
-            q_out = out_pool.tile([P, PAIR, C], F32)
-            k_out = out_pool.tile([P, PAIR, C], F32)
-            v_out = out_pool.tile([P, PAIR, C], F32)
-            out_sb[pair] = (q_out, k_out, v_out)
+        groups = {}
+        for name in "qkv":
+            first = 0
+            for count in STORES:
+                for n in range(first, first + count):
+                    groups[name, n] = (first, count)
+                first += count
+
+        def output_tile(name, n):
+            first, count = groups[name, n]
+            if n == first:
+                out_tile = out_pool.tile([P, OUT_TILES, C], F32, tag=name + "_out")
+                out_sb[name, first] = out_tile
+            return out_sb[name, first][:, n - first, :]
 
         def sum_of_squares(n, which):
             if n not in sums:
@@ -208,9 +221,8 @@ def tile_multiheadassociativememory_pa_kernel(
             inv_norms[n] = inv_norm
 
         def scale(n):
-            pair, i = divmod(n, PAIR)
             for which in range(2):
-                out = out_sb[pair][which][:, i, :]
+                out = output_tile("qk"[which], n)
                 inv_norm = inv_norms[n][:, which : which + 1]
                 if n == N_TILES - 1 and which == 1:
                     nc.scalar.activation(out=out, in_=qk_ps[n][which][:], func=ACT.Copy, scale=inv_norm)
@@ -218,22 +230,20 @@ def tile_multiheadassociativememory_pa_kernel(
                     nc.vector.tensor_scalar_mul(out=out, in0=qk_ps[n][which][:], scalar1=inv_norm)
 
         def copy_v(copy, n, v_ps):
-            pair, i = divmod(n, PAIR)
-            copy(out=out_sb[pair][2][:, i, :], in_=v_ps[:])
+            copy(out=output_tile("v", n), in_=v_ps[:])
 
-        def store(n, count, names="vqk"):
-            tiles = slice(n + 1 - count, n + 1)
-            part = slice(n % PAIR + 1 - count, n % PAIR + 1)
+        def store(n, names):
             for name in names:
-                rows, which = {"q": (q_rows, 0), "k": (k_rows, 1), "v": (v_rows, 2)}[name]
-                nc.sync.dma_start(out=rows[:, tiles, :], in_=out_sb[n // PAIR][which][:, part, :])
+                first, count = groups[name, n]
+                if n == first + count - 1:
+                    rows = {"q": q_rows, "k": k_rows, "v": v_rows}[name]
+                    nc.sync.dma_start(out=rows[:, first : n + 1, :], in_=out_sb[name, first][:, :count, :])
 
         def load_late_x():
             if late_loads:
                 load_x(late_loads[0], X_LOAD_TILES)
                 late_loads.remove(late_loads[0])
 
-        open_pair(0)
         first_q = [product(qk_psum, "q", q_mx, n) for n in range(PAIR)]
         turned = transpose_pair(1)
         v_ps = product(short_psum, "short", v_mx, 0)
@@ -245,11 +255,11 @@ def tile_multiheadassociativememory_pa_kernel(
         x_grouped = regroup_pair(turned, nc.scalar.copy)
         x_mx[1] = quantise_pair(x_grouped)
         copy_v(nc.scalar.copy, 0, v_ps)
-        store(0, 1, "v")
+        store(0, "v")
         load_late_x()
         v_ps = product(short_psum, "short", v_mx, 1)
         copy_v(nc.vector.tensor_copy, 1, v_ps)
-        store(1, 1, "v")
+        store(1, "v")
         load_late_x()
         for n in range(PAIR):
             sum_of_squares(n, 1)
@@ -261,8 +271,6 @@ def tile_multiheadassociativememory_pa_kernel(
         for n in range(1, N_TILES + 1):
             pair, i = divmod(n, PAIR)
             if PAIR <= n < N_TILES:
-                if i == 0:
-                    open_pair(pair)
                 q_ps = product(qk_psum, "q", q_mx, n)
                 k_ps = product(qk_psum, "k", k_mx, n)
                 v_ps = product(short_psum, "short", v_mx, n)
@@ -287,11 +295,8 @@ def tile_multiheadassociativememory_pa_kernel(
                 for i in range(PAIR):
                     copy_v(nc.scalar.copy, n - 1 + i, last_v[i])
             scale(n - 1)
-            pair, i = divmod(n - 1, PAIR)
-            if pair == 0:
-                store(n - 1, 1, "qk")
+            if n - 1 < PAIR:
+                store(n - 1, "qk")
                 load_late_x()
-            elif pair == N_PAIRS - 1:
-                store(n - 1, 1)
-            elif i == PAIR - 1:
-                store(n - 1, PAIR)
+            else:
+                store(n - 1, "vqk")

from contextlib import ExitStack

import concourse.mybir as mybir
from concourse.masks import make_identity

F32 = mybir.dt.float32
BF16 = mybir.dt.bfloat16
U32 = mybir.dt.uint32
U8 = mybir.dt.uint8
FP8X4 = mybir.dt.float8_e4m3fn_x4
ALU = mybir.AluOpType
ACT = mybir.ActivationFunctionType

P = 128
PACK = 4
K = P * PACK
C = 512
R = 128
TOKENS = 4 * 1024
N_TILES = TOKENS // P
PAIR = 2
N_PAIRS = N_TILES // PAIR
OUT_TILES = 2
STORES = [1, 1] + 15 * [OUT_TILES]
AHEAD = 2
X_LOAD_TILES = 8
X_EARLY_TILES = 24
V_ON_VECTOR = 8
EPS = 1e-12

FLOPS = 3 * 2 * TOKENS * K * C + 2 * K * C * R


def tile_multiheadassociativememory_pa_kernel(
    tc, x, basis, shared_q_w, shared_k_w, v_coeffs, out_0, out_1, out_2
):
    nc = tc.nc

    x_rows = x.flatten_outer_dims().rearrange("(p n) k -> p n k", n=N_TILES)
    q_rows = out_0.flatten_outer_dims().rearrange("(p n) c -> p n c", n=N_TILES)
    k_rows = out_1.flatten_outer_dims().rearrange("(p n) c -> p n c", n=N_TILES)
    v_rows = out_2.flatten_outer_dims().rearrange("(p n) c -> p n c", n=N_TILES)

    with ExitStack() as ctx:
        keep = ctx.enter_context(tc.tile_pool(name="keep", bufs=1))
        xq_pool = ctx.enter_context(tc.tile_pool(name="xq", bufs=AHEAD + 2))
        out_pool = ctx.enter_context(tc.tile_pool(name="outp", bufs=10))
        square_pool = ctx.enter_context(tc.tile_pool(name="square", bufs=16))
        norm_pool = ctx.enter_context(tc.tile_pool(name="norm", bufs=N_TILES))
        qk_psum = ctx.enter_context(tc.psum_pool(name="qk", bufs=3))
        short_psum = ctx.enter_context(tc.psum_pool(name="short", bufs=2))
        ctx.enter_context(tc.manual_schedule())

        def load_k_rows(rows, width, name):
            raw = keep.tile([P, PACK, width], BF16, name=name)
            nc.sync.dma_start(out=raw[:], in_=rows.rearrange("(p t) w -> p t w", t=PACK))
            return raw

        basis_sb = load_k_rows(basis, R, "basis_sb")
        coeff_sb = keep.tile([P, PACK, R], BF16)
        nc.sync.dma_start(out=coeff_sb[:], in_=v_coeffs.rearrange("(p a) r -> p a r", a=PACK))
        x_sb = {}

        def load_x(first, count):
            x_part = keep.tile([P, count * K], BF16, name="x_sb%d" % first)
            nc.sync.dma_start(
                out=x_part[:].rearrange("p (n k) -> p n k", k=K),
                in_=x_rows[:, first : first + count, :],
            )
            for n in range(count):
                x_sb[first + n] = (x_part, n)

        q_raw = load_k_rows(shared_q_w, C, "q_raw")
        load_x(0, PAIR)
        k_raw = load_k_rows(shared_k_w, C, "k_raw")
        load_x(PAIR, PAIR)
        load_x(2 * PAIR, X_LOAD_TILES - 2 * PAIR)
        for first in range(X_LOAD_TILES, X_EARLY_TILES, X_LOAD_TILES):
            load_x(first, X_LOAD_TILES)
        late_loads = list(range(X_EARLY_TILES, N_TILES, X_LOAD_TILES))

        ident_bf16 = keep.tile([P, P], BF16)
        make_identity(nc, ident_bf16[:])
        ident_f32 = keep.tile([P, P], F32)
        make_identity(nc, ident_f32[:])
        minus_half = keep.tile([P, 2], F32)
        nc.gpsimd.memset(minus_half[:], -0.5)

        def transpose_pair(pair):
            turned = short_psum.tile([P, PAIR * 2 * P], F32, tag="short")
            for i in range(PAIR):
                n = pair * PAIR + i
                x_part, place = x_sb[n]
                words = x_part[:].bitcast(F32)
                first = place * (K // 2)
                for u in range(2):
                    nc.tensor.transpose(
                        turned[:, (2 * i + u) * P : (2 * i + u + 1) * P],
                        words[:, first + u : first + 2 * P : 2],
                        ident_f32[:],
                    )
            return turned

        def regroup_pair(turned, copy):
            grouped = xq_pool.tile([P, PAIR * P * PACK], BF16, align_bytes=64, name="x_grouped")
            copy(
                out=grouped[:].bitcast(F32).rearrange("p (i r u) -> p i r u", i=PAIR, u=2),
                in_=turned[:].rearrange("p (i u r) -> p i r u", i=PAIR, u=2),
            )
            return grouped

        def quantise_pair(grouped):
            codes = xq_pool.tile([P, PAIR * P], U32, align_bytes=64, name="x_codes")
            scales = xq_pool.tile([P, PAIR * P], U8, align_bytes=64, name="x_scales")
            nc.vector.quantize_mx(out=codes[:].bitcast(FP8X4), scales=scales[:], in_=grouped[:])
            return codes, scales

        def regroup_weight(raw, name):
            grouped = keep.tile([P, C, PACK], BF16, align_bytes=64, name=name)
            nc.vector.tensor_copy(
                out=grouped[:].rearrange("p (c i) t -> p c t i", i=4),
                in_=raw[:].rearrange("p t (c i) -> p c t i", i=4),
            )
            return grouped

        def quantise_weight(grouped, name):
            codes = keep.tile([P, C], U32, align_bytes=64, name=name + "_codes")
            scales = keep.tile([P, C], U8, align_bytes=64, name=name + "_scales")
            nc.vector.quantize_mx(
                out=codes[:].bitcast(FP8X4),
                scales=scales[:],
                in_=grouped[:].rearrange("p c t -> p (c t)"),
            )
            return codes, scales

        basis_ps = qk_psum.tile([P, PACK, P], BF16, tag="q")
        for t in range(PACK):
            nc.tensor.transpose(basis_ps[:, t, :], basis_sb[:, t, :], ident_bf16[:])
        basis_turned = keep.tile([P, PACK, P], BF16)
        nc.vector.tensor_copy(out=basis_turned[:], in_=basis_ps[:])
        coeff_ps = short_psum.tile([P, PACK, P], BF16, tag="short")
        for a in range(PACK):
            nc.tensor.transpose(coeff_ps[:, a, :], coeff_sb[:, a, :], ident_bf16[:])
        coeff_turned = keep.tile([P, C], BF16)
        nc.vector.tensor_copy(
            out=coeff_turned[:].rearrange("p (c a) -> p c a", a=PACK), in_=coeff_ps[:].rearrange("p a c -> p c a")
        )

        v_grouped = keep.tile([P, C, PACK], BF16, align_bytes=64)
        for a in range(C // P):
            v_w_ps = qk_psum.tile([P, P, PACK], F32, tag="qk"[a % 2])
            for t in range(PACK):
                nc.tensor.matmul(
                    v_w_ps[:, :, t],
                    lhsT=basis_turned[:, t, :],
                    rhs=coeff_turned[:, a * P : (a + 1) * P],
                    start=True,
                    stop=True,
                )
            nc.scalar.copy(out=v_grouped[:, a * P : (a + 1) * P, :], in_=v_w_ps[:])
            if a == 0:
                x_grouped = regroup_pair(transpose_pair(0), nc.scalar.copy)

        x_mx = {}
        q_grouped = regroup_weight(q_raw, "q_grouped")
        q_mx = quantise_weight(q_grouped, "q")
        x_mx[0] = quantise_pair(x_grouped)
        k_grouped = regroup_weight(k_raw, "k_grouped")
        v_mx = quantise_weight(v_grouped, "v")
        k_mx = quantise_weight(k_grouped, "k")

        def product(psum, tag, weight_mx, n):
            codes, scales = x_mx[n // PAIR]
            cols = slice((n % PAIR) * P, (n % PAIR + 1) * P)
            acc = psum.tile([P, C], F32, tag=tag)
            nc.tensor.matmul_mx(
                out=acc[:],
                lhsT=codes[:, cols].bitcast(FP8X4),
                lhsT_scale=scales[:, cols],
                rhs=weight_mx[0][:].bitcast(FP8X4),
                rhs_scale=weight_mx[1][:],
                start=True,
                stop=True,
            )
            return acc

        out_sb = {}
        qk_ps = {}
        sums = {}
        inv_norms = {}

        groups = {}
        for name in "qkv":
            first = 0
            for count in STORES:
                for n in range(first, first + count):
                    groups[name, n] = (first, count)
                first += count

        def output_tile(name, n):
            first, count = groups[name, n]
            if n == first:
                out_tile = out_pool.tile([P, OUT_TILES, C], F32, tag=name + "_out")
                out_sb[name, first] = out_tile
            return out_sb[name, first][:, n - first, :]

        def sum_of_squares(n, which):
            if n not in sums:
                sumsq = norm_pool.tile([P, 2], F32)
                sums[n] = sumsq
            squares = square_pool.tile([P, C], BF16)
            nc.scalar.activation(
                out=squares[:], in_=qk_ps[n][which][:], func=ACT.Square, accum_out=sums[n][:, which : which + 1]
            )

        def invert_norms(n):
            bounded = norm_pool.tile([P, 2], F32)
            nc.gpsimd.tensor_scalar_max(out=bounded[:], in0=sums[n][:], scalar1=EPS * EPS)
            inv_norm = norm_pool.tile([P, 2], F32)
            nc.gpsimd.tensor_tensor(out=inv_norm[:], in0=bounded[:], in1=minus_half[:], op=ALU.pow)
            inv_norms[n] = inv_norm

        def scale(n):
            for which in range(2):
                out = output_tile("qk"[which], n)
                inv_norm = inv_norms[n][:, which : which + 1]
                if n == N_TILES - 1 and which == 1:
                    nc.scalar.activation(out=out, in_=qk_ps[n][which][:], func=ACT.Copy, scale=inv_norm)
                else:
                    nc.vector.tensor_scalar_mul(out=out, in0=qk_ps[n][which][:], scalar1=inv_norm)

        def copy_v(copy, n, v_ps):
            copy(out=output_tile("v", n), in_=v_ps[:])

        def store(n, names):
            for name in names:
                first, count = groups[name, n]
                if n == first + count - 1:
                    rows = {"q": q_rows, "k": k_rows, "v": v_rows}[name]
                    nc.sync.dma_start(out=rows[:, first : n + 1, :], in_=out_sb[name, first][:, :count, :])

        def load_late_x():
            if late_loads:
                load_x(late_loads[0], X_LOAD_TILES)
                late_loads.remove(late_loads[0])

        first_q = [product(qk_psum, "q", q_mx, n) for n in range(PAIR)]
        turned = transpose_pair(1)
        v_ps = product(short_psum, "short", v_mx, 0)
        first_k = [product(qk_psum, "k", k_mx, n) for n in range(PAIR)]
        for n in range(PAIR):
            qk_ps[n] = (first_q[n], first_k[n])
        for n in range(PAIR):
            sum_of_squares(n, 0)
        x_grouped = regroup_pair(turned, nc.scalar.copy)
        x_mx[1] = quantise_pair(x_grouped)
        copy_v(nc.scalar.copy, 0, v_ps)
        store(0, "v")
        load_late_x()
        v_ps = product(short_psum, "short", v_mx, 1)
        copy_v(nc.vector.tensor_copy, 1, v_ps)
        store(1, "v")
        load_late_x()
        for n in range(PAIR):
            sum_of_squares(n, 1)
            invert_norms(n)
        x_grouped = regroup_pair(transpose_pair(AHEAD), nc.vector.tensor_copy)
        x_mx[AHEAD] = quantise_pair(x_grouped)

        last_v = []
        for n in range(1, N_TILES + 1):
            pair, i = divmod(n, PAIR)
            if PAIR <= n < N_TILES:
                q_ps = product(qk_psum, "q", q_mx, n)
                k_ps = product(qk_psum, "k", k_mx, n)
                v_ps = product(short_psum, "short", v_mx, n)
                qk_ps[n] = (q_ps, k_ps)
                if i == 0 and pair + AHEAD < N_PAIRS:
                    turned = transpose_pair(pair + AHEAD)
                sum_of_squares(n, 0)
                sum_of_squares(n, 1)
                invert_norms(n)
                if pair == N_PAIRS - 1:
                    last_v.append(v_ps)
                elif n % V_ON_VECTOR == V_ON_VECTOR - 1:
                    copy_v(nc.vector.tensor_copy, n, v_ps)
                else:
                    copy_v(nc.scalar.copy, n, v_ps)
                if pair + AHEAD < N_PAIRS:
                    if i == 0:
                        x_grouped = regroup_pair(turned, nc.vector.tensor_copy)
                    else:
                        x_mx[pair + AHEAD] = quantise_pair(x_grouped)
            if n == N_TILES - 1:
                for i in range(PAIR):
                    copy_v(nc.scalar.copy, n - 1 + i, last_v[i])
            scale(n - 1)
            if n - 1 < PAIR:
                store(n - 1, "qk")
                load_late_x()
            else:
                store(n - 1, "vqk")
